import numpy as np
import ml_dtypes

BF16 = ml_dtypes.bfloat16


def bf(x):
    return np.asarray(x, np.float32).astype(BF16)


def f32(x):
    return np.asarray(x, np.float32)


def f64(x):
    return np.asarray(x).astype(np.float64)


def striped(idx):
    return np.tile(idx.reshape(-1, 16).T, (8, 1))


D, M, S, N = 128, 128, 2048, 1024


def setup_inputs():
    return {"table": bf(np.abs(np.random.standard_normal((D, S)))), "v": bf(0.05 * np.random.standard_normal((D, M))), "gain": f32(1.0 + 0.2 * np.random.standard_normal((M, 1))), "offs": striped(np.random.permutation(S)[:N])}


def reference(table, v, gain, offs):
    idx = offs[:16].T.reshape(-1)
    vv = f64(v)
    scale = f64(gain) / np.sqrt((vv * vv).sum(0))[:, None]
    return np.maximum(scale * (vv.T @ f64(table)[:, idx]), 0.0)

@@ -1,0 +1,50 @@
+import concourse.mybir as mybir
+
+BF16, F32, U16 = mybir.dt.bfloat16, mybir.dt.float32, mybir.dt.uint16
+MULT, MAX = mybir.AluOpType.mult, mybir.AluOpType.max
+SQRT = mybir.ActivationFunctionType.Sqrt
+
+K = 128
+M = 128
+S = 2048
+N = 1024
+PIECE = 256
+DMA_BLOCK = 256
+PER_COLUMN = 16
+
+FLOPS = 2 * K * M * N
+
+
+def tile_qnetwork_kernel(tc, table, v, gain, offs, out):
+    nc = tc.nc
+    with tc.tile_pool(name="held", bufs=1) as held, tc.psum_pool(name="psum", bufs=1) as psum:
+        nodes = held.tile([K, S], BF16, name="nodes")
+        nc.scalar.dma_start(nodes[:], table)
+        weights = held.tile([K, M], BF16, name="weights")
+        nc.sync.dma_start(weights[:], v)
+        offsets = held.tile([K, N // PER_COLUMN], U16, name="offsets")
+        nc.sync.dma_start(offsets[:], offs)
+        gain_col = held.tile([M, 1], F32, name="gain_col")
+        nc.scalar.dma_start(gain_col[:], gain)
+
+        squares = held.tile([K, M], F32, name="squares")
+        nc.vector.tensor_tensor(squares[:], weights[:], weights[:], MULT)
+        ones = held.tile([K, 1], F32, name="ones")
+        nc.vector.memset(ones[:], 1.0)
+        sum_squares = psum.tile([M, 1], F32, name="sum_squares")
+        nc.tensor.matmul(sum_squares[:], squares[:], ones[:], start=True, stop=True)
+        length = held.tile([M, 1], F32, name="length")
+        nc.scalar.activation(length[:], sum_squares[:], SQRT)
+        inverse_length = held.tile([M, 1], F32, name="inverse_length")
+        nc.vector.reciprocal(inverse_length[:], length[:])
+        scale = held.tile([M, 1], F32, name="scale")
+        nc.vector.tensor_tensor(scale[:], inverse_length[:], gain_col[:], MULT)
+
+        for piece in range(N // PIECE):
+            first = piece * PIECE
+            looked_up = nodes[:].indirect(offsets[:, first // PER_COLUMN : (first + PIECE) // PER_COLUMN])
+            projected = psum.tile([M, PIECE], F32, name=f"projected{piece}")
+            nc.tensor.matmul(projected[:], weights[:], looked_up, start=True, stop=True)
+            result = held.tile([M, PIECE], F32, name=f"result{piece}", align_bytes=DMA_BLOCK)
+            nc.vector.tensor_scalar(result[:], projected[:], scale[:], 0.0, MULT, MAX)
+            nc.sync.dma_start(out[:, first : first + PIECE], result[:])

@@ -2,13 +2,15 @@ import concourse.mybir as mybir
 
 BF16, F32, U16 = mybir.dt.bfloat16, mybir.dt.float32, mybir.dt.uint16
 MULT, MAX = mybir.AluOpType.mult, mybir.AluOpType.max
-SQRT = mybir.ActivationFunctionType.Sqrt
+RELU, SQRT = mybir.ActivationFunctionType.Relu, mybir.ActivationFunctionType.Sqrt
 
 K = 128
 M = 128
 S = 2048
 N = 1024
 PIECE = 256
+HALF = PIECE // 2
+PSUM_BANKS = 8
 DMA_BLOCK = 256
 PER_COLUMN = 16
 
@@ -17,7 +19,7 @@ FLOPS = 2 * K * M * N
 
 def tile_qnetwork_kernel(tc, table, v, gain, offs, out):
     nc = tc.nc
-    with tc.tile_pool(name="held", bufs=1) as held, tc.psum_pool(name="psum", bufs=1) as psum:
+    with tc.tile_pool(name="held", bufs=1) as held, tc.psum_pool(name="psum", bufs=PSUM_BANKS) as psum:
         nodes = held.tile([K, S], BF16, name="nodes")
         nc.scalar.dma_start(nodes[:], table)
         weights = held.tile([K, M], BF16, name="weights")
@@ -31,7 +33,7 @@ def tile_qnetwork_kernel(tc, table, v, gain, offs, out):
         nc.vector.tensor_tensor(squares[:], weights[:], weights[:], MULT)
         ones = held.tile([K, 1], F32, name="ones")
         nc.vector.memset(ones[:], 1.0)
-        sum_squares = psum.tile([M, 1], F32, name="sum_squares")
+        sum_squares = psum.tile([M, 1], F32, name="sum_squares", tag="bank")
         nc.tensor.matmul(sum_squares[:], squares[:], ones[:], start=True, stop=True)
         length = held.tile([M, 1], F32, name="length")
         nc.scalar.activation(length[:], sum_squares[:], SQRT)
@@ -42,9 +44,15 @@ def tile_qnetwork_kernel(tc, table, v, gain, offs, out):
 
         for piece in range(N // PIECE):
             first = piece * PIECE
-            looked_up = nodes[:].indirect(offsets[:, first // PER_COLUMN : (first + PIECE) // PER_COLUMN])
-            projected = psum.tile([M, PIECE], F32, name=f"projected{piece}")
-            nc.tensor.matmul(projected[:], weights[:], looked_up, start=True, stop=True)
             result = held.tile([M, PIECE], F32, name=f"result{piece}", align_bytes=DMA_BLOCK)
-            nc.vector.tensor_scalar(result[:], projected[:], scale[:], 0.0, MULT, MAX)
+            for half in range(PIECE // HALF):
+                entry = first + half * HALF
+                looked_up = nodes[:].indirect(offsets[:, entry // PER_COLUMN : (entry + HALF) // PER_COLUMN])
+                projected = psum.tile([M, HALF], F32, name=f"projected{entry // HALF}", tag="bank")
+                nc.tensor.matmul(projected[:], weights[:], looked_up, start=True, stop=True)
+                columns = result[:, half * HALF : (half + 1) * HALF]
+                if half == 0:
+                    nc.vector.tensor_scalar(columns, projected[:], scale[:], 0.0, MULT, MAX)
+                else:
+                    nc.scalar.activation(columns, projected[:], RELU, scale=scale[:])
             nc.sync.dma_start(out[:, first : first + PIECE], result[:])

import concourse.mybir as mybir

BF16, F32, U16 = mybir.dt.bfloat16, mybir.dt.float32, mybir.dt.uint16
MULT, MAX = mybir.AluOpType.mult, mybir.AluOpType.max
RELU, SQRT = mybir.ActivationFunctionType.Relu, mybir.ActivationFunctionType.Sqrt

K = 128
M = 128
S = 2048
N = 1024
PIECE = 256
HALF = PIECE // 2
PSUM_BANKS = 8
DMA_BLOCK = 256
PER_COLUMN = 16

FLOPS = 2 * K * M * N


def tile_qnetwork_kernel(tc, table, v, gain, offs, out):
    nc = tc.nc
    with tc.tile_pool(name="held", bufs=1) as held, tc.psum_pool(name="psum", bufs=PSUM_BANKS) as psum:
        nodes = held.tile([K, S], BF16, name="nodes")
        nc.scalar.dma_start(nodes[:], table)
        weights = held.tile([K, M], BF16, name="weights")
        nc.sync.dma_start(weights[:], v)
        offsets = held.tile([K, N // PER_COLUMN], U16, name="offsets")
        nc.sync.dma_start(offsets[:], offs)
        gain_col = held.tile([M, 1], F32, name="gain_col")
        nc.scalar.dma_start(gain_col[:], gain)

        squares = held.tile([K, M], F32, name="squares")
        nc.vector.tensor_tensor(squares[:], weights[:], weights[:], MULT)
        ones = held.tile([K, 1], F32, name="ones")
        nc.vector.memset(ones[:], 1.0)
        sum_squares = psum.tile([M, 1], F32, name="sum_squares", tag="bank")
        nc.tensor.matmul(sum_squares[:], squares[:], ones[:], start=True, stop=True)
        length = held.tile([M, 1], F32, name="length")
        nc.scalar.activation(length[:], sum_squares[:], SQRT)
        inverse_length = held.tile([M, 1], F32, name="inverse_length")
        nc.vector.reciprocal(inverse_length[:], length[:])
        scale = held.tile([M, 1], F32, name="scale")
        nc.vector.tensor_tensor(scale[:], inverse_length[:], gain_col[:], MULT)

        for piece in range(N // PIECE):
            first = piece * PIECE
            result = held.tile([M, PIECE], F32, name=f"result{piece}", align_bytes=DMA_BLOCK)
            for half in range(PIECE // HALF):
                entry = first + half * HALF
                looked_up = nodes[:].indirect(offsets[:, entry // PER_COLUMN : (entry + HALF) // PER_COLUMN])
                projected = psum.tile([M, HALF], F32, name=f"projected{entry // HALF}", tag="bank")
                nc.tensor.matmul(projected[:], weights[:], looked_up, start=True, stop=True)
                columns = result[:, half * HALF : (half + 1) * HALF]
                if half == 0:
                    nc.vector.tensor_scalar(columns, projected[:], scale[:], 0.0, MULT, MAX)
                else:
                    nc.scalar.activation(columns, projected[:], RELU, scale=scale[:])
            nc.sync.dma_start(out[:, first : first + PIECE], result[:])
